import numpy as np
import ml_dtypes

BF16 = ml_dtypes.bfloat16


def bf(x):
    return np.asarray(x, np.float32).astype(BF16)


def f32(x):
    return np.asarray(x, np.float32)


def f64(x):
    return np.asarray(x).astype(np.float64)


def striped(idx):
    return np.tile(idx.reshape(-1, 16).T, (8, 1))


C, F, S, N = 256, 1024, 4096, 512
EPS = 1e-5
ERF_LIM, ERF_TERMS = 6.0, 150


def erf(a):
    a = np.asarray(a, np.float64)
    c = np.clip(a, -ERF_LIM, ERF_LIM)
    term = c.copy()
    total = c.copy()
    for n in range(1, ERF_TERMS):
        term = term * 2.0 * c * c / (2.0 * n + 1.0)
        total = total + term
    r = 2.0 / np.sqrt(np.pi) * np.exp(-c * c) * total
    return np.where(np.abs(a) > ERF_LIM, np.sign(a), r)


def gelu_erf(v):
    return 0.5 * v * (1.0 + erf(v / np.sqrt(2.0)))


def setup_inputs():
    return {"base": f32(np.random.standard_normal((C, S))), "x": bf(np.random.standard_normal((C, N))), "w1": bf(np.random.standard_normal((C, F)) / np.sqrt(C)), "b1": f32(0.1 * np.random.standard_normal((F, 1))), "w2": bf(np.random.standard_normal((F, C)) / np.sqrt(F)), "b2": f32(0.1 * np.random.standard_normal((C, 1))), "ln_w": f32(1.0 + 0.1 * np.random.standard_normal((C, 1))), "ln_b": f32(0.1 * np.random.standard_normal((C, 1))), "offs": striped(np.random.permutation(S)[:N])}


def reference(base, x, w1, b1, w2, b2, ln_w, ln_b, offs):
    idx = offs[:16].T.reshape(-1)
    h = gelu_erf(f64(w1).T @ f64(x) + f64(b1))
    y = f64(w2).T @ h + f64(b2)
    mu = y.mean(axis=0, keepdims=True)
    var = ((y - mu) ** 2).mean(axis=0, keepdims=True)
    z = (y - mu) / np.sqrt(var + EPS) * f64(ln_w) + f64(ln_b)
    out = f64(base).copy()
    out[:, idx] = f64(x) + z
    return out

@@ -1,0 +1,103 @@
+import concourse.mybir as mybir
+from concourse.masks import make_identity
+
+P = 128
+C, F, S, N = 256, 1024, 4096, 512
+CB, FB, JB = C // P, F // P, N // P
+EPS = 1e-5
+FLOPS = 2 * C * F * N * 2
+
+BF16, F32, U16 = mybir.dt.bfloat16, mybir.dt.float32, mybir.dt.uint16
+ADD, SUB, MULT = mybir.AluOpType.add, mybir.AluOpType.subtract, mybir.AluOpType.mult
+ACT = mybir.ActivationFunctionType
+
+
+def tile_gridtransformerblock_kernel(tc, base, x, w1, b1, w2, b2, ln_w, ln_b, offs, out):
+    nc = tc.nc
+    with (
+        tc.tile_pool(name="held", bufs=1) as held,
+        tc.tile_pool(name="work", bufs=2) as work,
+        tc.psum_pool(name="psum_h", bufs=3) as psum_h,
+        tc.psum_pool(name="psum_y", bufs=2) as psum_y,
+        tc.psum_pool(name="psum_z", bufs=2) as psum_z,
+    ):
+        offsets = held.tile([P, N // 16], U16, name="offsets")
+        nc.sync.dma_start(offsets[:], offs)
+        x_bf = held.tile([P, CB, N], BF16, name="x_bf")
+        nc.sync.dma_start(x_bf[:], x.rearrange("(cb p) n -> p cb n", p=P))
+        w1_sb = held.tile([P, CB, F], BF16, name="w1_sb")
+        nc.sync.dma_start(w1_sb[:], w1.rearrange("(cb p) f -> p cb f", p=P))
+        w2_sb = held.tile([P, FB, C], BF16, name="w2_sb")
+        nc.sync.dma_start(w2_sb[:], w2.rearrange("(fb p) c -> p fb c", p=P))
+        window = [held.tile([P, S], F32, name=f"window{cb}") for cb in range(CB)]
+        for cb in range(CB):
+            nc.sync.dma_start(window[cb][:], base[cb * P : (cb + 1) * P, :])
+
+        b1_col = held.tile([P, FB], F32, name="b1_col")
+        ln_w_col = held.tile([P, CB], F32, name="ln_w_col")
+        ln_b_col = held.tile([P, CB], F32, name="ln_b_col")
+        b2_row = held.tile([P, C], F32, name="b2_row")
+        with nc.allow_non_contiguous_dma(reason="one float32 to a partition: small vectors"):
+            nc.scalar.dma_start(b1_col[:], b1.rearrange("(fb p) o -> p (fb o)", p=P))
+            nc.scalar.dma_start(ln_w_col[:], ln_w.rearrange("(cb p) o -> p (cb o)", p=P))
+            nc.scalar.dma_start(ln_b_col[:], ln_b.rearrange("(cb p) o -> p (cb o)", p=P))
+        nc.scalar.dma_start(b2_row[:], b2.rearrange("c o -> (c o)").partition_broadcast(P))
+
+        identity = held.tile([P, P], F32, name="identity")
+        make_identity(nc, identity[:])
+        eps_col = held.tile([P, 1], F32, name="eps_col")
+        nc.vector.memset(eps_col[:], EPS)
+
+        x_f32 = [held.tile([P, N], F32, name=f"x_f32_{cb}") for cb in range(CB)]
+        for cb in range(CB):
+            nc.gpsimd.tensor_copy(x_f32[cb][:], x_bf[:, cb, :])
+
+        h = held.tile([P, FB, N], BF16, name="h")
+        for fb in range(FB):
+            h_ps = psum_h.tile([P, N], F32, name="h_ps")
+            for cb in range(CB):
+                nc.tensor.matmul(
+                    h_ps[:],
+                    w1_sb[:, cb, fb * P : (fb + 1) * P],
+                    x_bf[:, cb, :],
+                    start=(cb == 0),
+                    stop=(cb == CB - 1),
+                )
+            nc.scalar.activation(h[:, fb, :], h_ps[:], ACT.Gelu, bias=b1_col[:, fb : fb + 1])
+
+        z = [held.tile([P, N], F32, name=f"z{cb}") for cb in range(CB)]
+        for jb in range(JB):
+            pixels = slice(jb * P, (jb + 1) * P)
+            y_ps = psum_y.tile([P, C], F32, name="y_ps")
+            for fb in range(FB):
+                nc.tensor.matmul(
+                    y_ps[:], h[:, fb, pixels], w2_sb[:, fb, :], start=(fb == 0), stop=(fb == FB - 1)
+                )
+            y_sb = work.tile([P, C], F32, name="y_sb")
+            nc.vector.tensor_tensor(y_sb[:], y_ps[:], b2_row[:], ADD)
+
+            stats = work.tile([P, 6], F32, name="stats")
+            nc.vector.bn_stats(stats[:], y_sb[:])
+            mean_var = work.tile([P, 2], F32, name="mean_var")
+            nc.vector.bn_aggr(mean_var[:], stats[:])
+            std = work.tile([P, 1], F32, name="std")
+            nc.scalar.activation(std[:], mean_var[:, 1:2], ACT.Sqrt, bias=eps_col[:, 0:1])
+            rstd = work.tile([P, 1], F32, name="rstd")
+            nc.vector.reciprocal(rstd[:], std[:])
+            normed = work.tile([P, C], F32, name="normed")
+            nc.vector.tensor_scalar(normed[:], y_sb[:], mean_var[:, 0:1], rstd[:, 0:1], SUB, MULT)
+
+            z_ps = psum_z.tile([P, CB, P], F32, name="z_ps")
+            for cb in range(CB):
+                nc.tensor.transpose(z_ps[:, cb, :], normed[:, cb * P : (cb + 1) * P], identity[:])
+                nc.scalar.activation(
+                    z[cb][:, pixels],
+                    z_ps[:, cb, :],
+                    ACT.Identity,
+                    scale=ln_w_col[:, cb : cb + 1],
+                    bias=ln_b_col[:, cb : cb + 1],
+                )
+
+        for cb in range(CB):
+            nc.vector.tensor_tensor(window[cb][:].indirect(offsets[:]), x_f32[cb][:], z[cb][:], ADD)
+            nc.sync.dma_start(out[cb * P : (cb + 1) * P, :], window[cb][:])

@@ -16,7 +16,7 @@ def tile_gridtransformerblock_kernel(tc, base, x, w1, b1, w2, b2, ln_w, ln_b, of
     nc = tc.nc
     with (
         tc.tile_pool(name="held", bufs=1) as held,
-        tc.tile_pool(name="work", bufs=2) as work,
+        tc.tile_pool(name="work", bufs=JB) as work,
         tc.psum_pool(name="psum_h", bufs=3) as psum_h,
         tc.psum_pool(name="psum_y", bufs=2) as psum_y,
         tc.psum_pool(name="psum_z", bufs=2) as psum_z,
@@ -66,37 +66,54 @@ def tile_gridtransformerblock_kernel(tc, base, x, w1, b1, w2, b2, ln_w, ln_b, of
             nc.scalar.activation(h[:, fb, :], h_ps[:], ACT.Gelu, bias=b1_col[:, fb : fb + 1])
 
         z = [held.tile([P, N], F32, name=f"z{cb}") for cb in range(CB)]
-        for jb in range(JB):
-            pixels = slice(jb * P, (jb + 1) * P)
+        y_sb, mean_var, std, normed = {}, {}, {}, {}
+
+        def second_matmul_and_statistics(jb):
             y_ps = psum_y.tile([P, C], F32, name="y_ps")
             for fb in range(FB):
                 nc.tensor.matmul(
-                    y_ps[:], h[:, fb, pixels], w2_sb[:, fb, :], start=(fb == 0), stop=(fb == FB - 1)
+                    y_ps[:],
+                    h[:, fb, jb * P : (jb + 1) * P],
+                    w2_sb[:, fb, :],
+                    start=(fb == 0),
+                    stop=(fb == FB - 1),
                 )
-            y_sb = work.tile([P, C], F32, name="y_sb")
-            nc.vector.tensor_tensor(y_sb[:], y_ps[:], b2_row[:], ADD)
-
+            y_sb[jb] = work.tile([P, C], F32, name="y_sb")
+            nc.vector.tensor_tensor(y_sb[jb][:], y_ps[:], b2_row[:], ADD)
             stats = work.tile([P, 6], F32, name="stats")
-            nc.vector.bn_stats(stats[:], y_sb[:])
-            mean_var = work.tile([P, 2], F32, name="mean_var")
-            nc.vector.bn_aggr(mean_var[:], stats[:])
-            std = work.tile([P, 1], F32, name="std")
-            nc.scalar.activation(std[:], mean_var[:, 1:2], ACT.Sqrt, bias=eps_col[:, 0:1])
-            rstd = work.tile([P, 1], F32, name="rstd")
-            nc.vector.reciprocal(rstd[:], std[:])
-            normed = work.tile([P, C], F32, name="normed")
-            nc.vector.tensor_scalar(normed[:], y_sb[:], mean_var[:, 0:1], rstd[:, 0:1], SUB, MULT)
+            nc.vector.bn_stats(stats[:], y_sb[jb][:])
+            mean_var[jb] = work.tile([P, 2], F32, name="mean_var")
+            nc.vector.bn_aggr(mean_var[jb][:], stats[:])
+            std[jb] = work.tile([P, 1], F32, name="std")
+            nc.scalar.activation(std[jb][:], mean_var[jb][:, 1:2], ACT.Sqrt, bias=eps_col[:, 0:1])
 
+        def normalise(jb):
+            rstd = work.tile([P, 1], F32, name="rstd")
+            nc.vector.reciprocal(rstd[:], std[jb][:])
+            normed[jb] = work.tile([P, C], F32, name="normed")
+            nc.vector.tensor_scalar(
+                normed[jb][:], y_sb[jb][:], mean_var[jb][:, 0:1], rstd[:, 0:1], SUB, MULT
+            )
+
+        def back_to_channels(jb):
             z_ps = psum_z.tile([P, CB, P], F32, name="z_ps")
             for cb in range(CB):
-                nc.tensor.transpose(z_ps[:, cb, :], normed[:, cb * P : (cb + 1) * P], identity[:])
+                nc.tensor.transpose(z_ps[:, cb, :], normed[jb][:, cb * P : (cb + 1) * P], identity[:])
                 nc.scalar.activation(
-                    z[cb][:, pixels],
+                    z[cb][:, jb * P : (jb + 1) * P],
                     z_ps[:, cb, :],
                     ACT.Identity,
                     scale=ln_w_col[:, cb : cb + 1],
                     bias=ln_b_col[:, cb : cb + 1],
                 )
+
+        for step in range(JB + 2):
+            if step < JB:
+                second_matmul_and_statistics(step)
+            if 1 <= step <= JB:
+                normalise(step - 1)
+            if step >= 2:
+                back_to_channels(step - 2)
 
         for cb in range(CB):
             nc.vector.tensor_tensor(window[cb][:].indirect(offsets[:]), x_f32[cb][:], z[cb][:], ADD)

@@ -6,6 +6,7 @@ C, F, S, N = 256, 1024, 4096, 512
 CB, FB, JB = C // P, F // P, N // P
 EPS = 1e-5
 FLOPS = 2 * C * F * N * 2
+WARM_UP_MATMULS = 8
 
 BF16, F32, U16 = mybir.dt.bfloat16, mybir.dt.float32, mybir.dt.uint16
 ADD, SUB, MULT = mybir.AluOpType.add, mybir.AluOpType.subtract, mybir.AluOpType.mult
@@ -16,19 +17,30 @@ def tile_gridtransformerblock_kernel(tc, base, x, w1, b1, w2, b2, ln_w, ln_b, of
     nc = tc.nc
     with (
         tc.tile_pool(name="held", bufs=1) as held,
-        tc.tile_pool(name="work", bufs=JB) as work,
+        tc.tile_pool(name="work", bufs=2) as work,
         tc.psum_pool(name="psum_h", bufs=3) as psum_h,
         tc.psum_pool(name="psum_y", bufs=2) as psum_y,
         tc.psum_pool(name="psum_z", bufs=2) as psum_z,
+        tc.psum_pool(name="psum_warm", bufs=1) as psum_warm,
     ):
-        offsets = held.tile([P, N // 16], U16, name="offsets")
-        nc.sync.dma_start(offsets[:], offs)
+        zeros = held.tile([P, N], BF16, name="zeros")
+        nc.vector.memset(zeros[:], 0.0)
+        warm_ps = psum_warm.tile([P, N], F32, name="warm_ps")
+        for repeat in range(WARM_UP_MATMULS):
+            nc.tensor.matmul(warm_ps[:], zeros[:, 0:P], zeros[:], start=True, stop=True)
+
+
         x_bf = held.tile([P, CB, N], BF16, name="x_bf")
         nc.sync.dma_start(x_bf[:], x.rearrange("(cb p) n -> p cb n", p=P))
         w1_sb = held.tile([P, CB, F], BF16, name="w1_sb")
-        nc.sync.dma_start(w1_sb[:], w1.rearrange("(cb p) f -> p cb f", p=P))
+        w1_view = w1.rearrange("(cb p) f -> p cb f", p=P)
+        for piece in range(FB // 2):
+            columns = slice(piece * 2 * P, (piece + 1) * 2 * P)
+            nc.sync.dma_start(w1_sb[:, :, columns], w1_view[:, :, columns])
         w2_sb = held.tile([P, FB, C], BF16, name="w2_sb")
         nc.sync.dma_start(w2_sb[:], w2.rearrange("(fb p) c -> p fb c", p=P))
+        offsets = held.tile([P, N // 16], U16, name="offsets")
+        nc.sync.dma_start(offsets[:], offs)
         window = [held.tile([P, S], F32, name=f"window{cb}") for cb in range(CB)]
         for cb in range(CB):
             nc.sync.dma_start(window[cb][:], base[cb * P : (cb + 1) * P, :])
@@ -66,54 +78,37 @@ def tile_gridtransformerblock_kernel(tc, base, x, w1, b1, w2, b2, ln_w, ln_b, of
             nc.scalar.activation(h[:, fb, :], h_ps[:], ACT.Gelu, bias=b1_col[:, fb : fb + 1])
 
         z = [held.tile([P, N], F32, name=f"z{cb}") for cb in range(CB)]
-        y_sb, mean_var, std, normed = {}, {}, {}, {}
-
-        def second_matmul_and_statistics(jb):
+        for jb in range(JB):
+            pixels = slice(jb * P, (jb + 1) * P)
             y_ps = psum_y.tile([P, C], F32, name="y_ps")
             for fb in range(FB):
                 nc.tensor.matmul(
-                    y_ps[:],
-                    h[:, fb, jb * P : (jb + 1) * P],
-                    w2_sb[:, fb, :],
-                    start=(fb == 0),
-                    stop=(fb == FB - 1),
+                    y_ps[:], h[:, fb, pixels], w2_sb[:, fb, :], start=(fb == 0), stop=(fb == FB - 1)
                 )
-            y_sb[jb] = work.tile([P, C], F32, name="y_sb")
-            nc.vector.tensor_tensor(y_sb[jb][:], y_ps[:], b2_row[:], ADD)
+            y_sb = work.tile([P, C], F32, name="y_sb")
+            nc.vector.tensor_tensor(y_sb[:], y_ps[:], b2_row[:], ADD)
+
             stats = work.tile([P, 6], F32, name="stats")
-            nc.vector.bn_stats(stats[:], y_sb[jb][:])
-            mean_var[jb] = work.tile([P, 2], F32, name="mean_var")
-            nc.vector.bn_aggr(mean_var[jb][:], stats[:])
-            std[jb] = work.tile([P, 1], F32, name="std")
-            nc.scalar.activation(std[jb][:], mean_var[jb][:, 1:2], ACT.Sqrt, bias=eps_col[:, 0:1])
-
-        def normalise(jb):
+            nc.vector.bn_stats(stats[:], y_sb[:])
+            mean_var = work.tile([P, 2], F32, name="mean_var")
+            nc.vector.bn_aggr(mean_var[:], stats[:])
+            std = work.tile([P, 1], F32, name="std")
+            nc.scalar.activation(std[:], mean_var[:, 1:2], ACT.Sqrt, bias=eps_col[:, 0:1])
             rstd = work.tile([P, 1], F32, name="rstd")
-            nc.vector.reciprocal(rstd[:], std[jb][:])
-            normed[jb] = work.tile([P, C], F32, name="normed")
-            nc.vector.tensor_scalar(
-                normed[jb][:], y_sb[jb][:], mean_var[jb][:, 0:1], rstd[:, 0:1], SUB, MULT
-            )
+            nc.vector.reciprocal(rstd[:], std[:])
+            normed = work.tile([P, C], F32, name="normed")
+            nc.vector.tensor_scalar(normed[:], y_sb[:], mean_var[:, 0:1], rstd[:, 0:1], SUB, MULT)
 
-        def back_to_channels(jb):
             z_ps = psum_z.tile([P, CB, P], F32, name="z_ps")
             for cb in range(CB):
-                nc.tensor.transpose(z_ps[:, cb, :], normed[jb][:, cb * P : (cb + 1) * P], identity[:])
+                nc.tensor.transpose(z_ps[:, cb, :], normed[:, cb * P : (cb + 1) * P], identity[:])
                 nc.scalar.activation(
-                    z[cb][:, jb * P : (jb + 1) * P],
+                    z[cb][:, pixels],
                     z_ps[:, cb, :],
                     ACT.Identity,
                     scale=ln_w_col[:, cb : cb + 1],
                     bias=ln_b_col[:, cb : cb + 1],
                 )
-
-        for step in range(JB + 2):
-            if step < JB:
-                second_matmul_and_statistics(step)
-            if 1 <= step <= JB:
-                normalise(step - 1)
-            if step >= 2:
-                back_to_channels(step - 2)
 
         for cb in range(CB):
             nc.vector.tensor_tensor(window[cb][:].indirect(offsets[:]), x_f32[cb][:], z[cb][:], ADD)

@@ -6,7 +6,8 @@ C, F, S, N = 256, 1024, 4096, 512
 CB, FB, JB = C // P, F // P, N // P
 EPS = 1e-5
 FLOPS = 2 * C * F * N * 2
-WARM_UP_MATMULS = 8
+WARM_UP_MATMULS = 4
+W1_FIRST = 2 * P
 
 BF16, F32, U16 = mybir.dt.bfloat16, mybir.dt.float32, mybir.dt.uint16
 ADD, SUB, MULT = mybir.AluOpType.add, mybir.AluOpType.subtract, mybir.AluOpType.mult
@@ -21,44 +22,43 @@ def tile_gridtransformerblock_kernel(tc, base, x, w1, b1, w2, b2, ln_w, ln_b, of
         tc.psum_pool(name="psum_h", bufs=3) as psum_h,
         tc.psum_pool(name="psum_y", bufs=2) as psum_y,
         tc.psum_pool(name="psum_z", bufs=2) as psum_z,
-        tc.psum_pool(name="psum_warm", bufs=1) as psum_warm,
     ):
-        zeros = held.tile([P, N], BF16, name="zeros")
-        nc.vector.memset(zeros[:], 0.0)
-        warm_ps = psum_warm.tile([P, N], F32, name="warm_ps")
-        for repeat in range(WARM_UP_MATMULS):
-            nc.tensor.matmul(warm_ps[:], zeros[:, 0:P], zeros[:], start=True, stop=True)
-
-
         x_bf = held.tile([P, CB, N], BF16, name="x_bf")
-        nc.sync.dma_start(x_bf[:], x.rearrange("(cb p) n -> p cb n", p=P))
         w1_sb = held.tile([P, CB, F], BF16, name="w1_sb")
-        w1_view = w1.rearrange("(cb p) f -> p cb f", p=P)
-        for piece in range(FB // 2):
-            columns = slice(piece * 2 * P, (piece + 1) * 2 * P)
-            nc.sync.dma_start(w1_sb[:, :, columns], w1_view[:, :, columns])
         w2_sb = held.tile([P, FB, C], BF16, name="w2_sb")
-        nc.sync.dma_start(w2_sb[:], w2.rearrange("(fb p) c -> p fb c", p=P))
         offsets = held.tile([P, N // 16], U16, name="offsets")
-        nc.sync.dma_start(offsets[:], offs)
         window = [held.tile([P, S], F32, name=f"window{cb}") for cb in range(CB)]
-        for cb in range(CB):
-            nc.sync.dma_start(window[cb][:], base[cb * P : (cb + 1) * P, :])
+        w1_view = w1.rearrange("(cb p) f -> p cb f", p=P)
+        nc.sync.dma_start(x_bf[:], x.rearrange("(cb p) n -> p cb n", p=P))
+        nc.scalar.dma_start(w1_sb[:, :, 0:W1_FIRST], w1_view[:, :, 0:W1_FIRST])
 
         b1_col = held.tile([P, FB], F32, name="b1_col")
         ln_w_col = held.tile([P, CB], F32, name="ln_w_col")
         ln_b_col = held.tile([P, CB], F32, name="ln_b_col")
         b2_row = held.tile([P, C], F32, name="b2_row")
-        with nc.allow_non_contiguous_dma(reason="one float32 to a partition: small vectors"):
-            nc.scalar.dma_start(b1_col[:], b1.rearrange("(fb p) o -> p (fb o)", p=P))
-            nc.scalar.dma_start(ln_w_col[:], ln_w.rearrange("(cb p) o -> p (cb o)", p=P))
-            nc.scalar.dma_start(ln_b_col[:], ln_b.rearrange("(cb p) o -> p (cb o)", p=P))
-        nc.scalar.dma_start(b2_row[:], b2.rearrange("c o -> (c o)").partition_broadcast(P))
-
+        with nc.allow_non_contiguous_dma(reason="small vectors, one float32 to a partition"):
+            nc.sync.dma_start(b1_col[:], b1.rearrange("(fb p) o -> p (fb o)", p=P))
+        nc.sync.dma_start(w1_sb[:, :, W1_FIRST:F], w1_view[:, :, W1_FIRST:F])
+        nc.sync.dma_start(w2_sb[:], w2.rearrange("(fb p) c -> p fb c", p=P))
+        nc.sync.dma_start(b2_row[:], b2.rearrange("c o -> (c o)").partition_broadcast(P))
+        with nc.allow_non_contiguous_dma(reason="small vectors, one float32 to a partition"):
+            nc.sync.dma_start(ln_w_col[:], ln_w.rearrange("(cb p) o -> p (cb o)", p=P))
+            nc.sync.dma_start(ln_b_col[:], ln_b.rearrange("(cb p) o -> p (cb o)", p=P))
+        nc.sync.dma_start(offsets[:], offs)
+        for cb in range(CB):
+            nc.sync.dma_start(window[cb][:], base[cb * P : (cb + 1) * P, :])
         identity = held.tile([P, P], F32, name="identity")
         make_identity(nc, identity[:])
+
+        zeros = held.tile([P, N], BF16, name="zeros")
+        nc.vector.memset(zeros[:], 0.0)
+        warm_ps = psum_h.tile([P, N], F32, name="warm_ps", tag="h_ps")
+        for repeat in range(WARM_UP_MATMULS):
+            nc.tensor.matmul(warm_ps[:], zeros[:, 0:P], zeros[:], start=True, stop=True)
         eps_col = held.tile([P, 1], F32, name="eps_col")
         nc.vector.memset(eps_col[:], EPS)
+        scratch_col = held.tile([P, 1], F32, name="scratch_col")
+        nc.scalar.activation(scratch_col[:], eps_col[:], ACT.Gelu)
 
         x_f32 = [held.tile([P, N], F32, name=f"x_f32_{cb}") for cb in range(CB)]
         for cb in range(CB):
@@ -92,10 +92,8 @@ def tile_gridtransformerblock_kernel(tc, base, x, w1, b1, w2, b2, ln_w, ln_b, of
             nc.vector.bn_stats(stats[:], y_sb[:])
             mean_var = work.tile([P, 2], F32, name="mean_var")
             nc.vector.bn_aggr(mean_var[:], stats[:])
-            std = work.tile([P, 1], F32, name="std")
-            nc.scalar.activation(std[:], mean_var[:, 1:2], ACT.Sqrt, bias=eps_col[:, 0:1])
             rstd = work.tile([P, 1], F32, name="rstd")
-            nc.vector.reciprocal(rstd[:], std[:])
+            nc.scalar.activation(rstd[:], mean_var[:, 1:2], ACT.Abs_reciprocal_sqrt, bias=eps_col[:, 0:1])
             normed = work.tile([P, C], F32, name="normed")
             nc.vector.tensor_scalar(normed[:], y_sb[:], mean_var[:, 0:1], rstd[:, 0:1], SUB, MULT)
 

@@ -6,8 +6,7 @@ C, F, S, N = 256, 1024, 4096, 512
 CB, FB, JB = C // P, F // P, N // P
 EPS = 1e-5
 FLOPS = 2 * C * F * N * 2
-WARM_UP_MATMULS = 4
-W1_FIRST = 2 * P
+WARM_UP_MATMULS = 5
 
 BF16, F32, U16 = mybir.dt.bfloat16, mybir.dt.float32, mybir.dt.uint16
 ADD, SUB, MULT = mybir.AluOpType.add, mybir.AluOpType.subtract, mybir.AluOpType.mult
@@ -24,22 +23,18 @@ def tile_gridtransformerblock_kernel(tc, base, x, w1, b1, w2, b2, ln_w, ln_b, of
         tc.psum_pool(name="psum_z", bufs=2) as psum_z,
     ):
         x_bf = held.tile([P, CB, N], BF16, name="x_bf")
-        w1_sb = held.tile([P, CB, F], BF16, name="w1_sb")
-        w2_sb = held.tile([P, FB, C], BF16, name="w2_sb")
-        offsets = held.tile([P, N // 16], U16, name="offsets")
-        window = [held.tile([P, S], F32, name=f"window{cb}") for cb in range(CB)]
-        w1_view = w1.rearrange("(cb p) f -> p cb f", p=P)
-        nc.sync.dma_start(x_bf[:], x.rearrange("(cb p) n -> p cb n", p=P))
-        nc.scalar.dma_start(w1_sb[:, :, 0:W1_FIRST], w1_view[:, :, 0:W1_FIRST])
-
+        w1_sb = held.tile([P, CB, P, FB], BF16, name="w1_sb")
         b1_col = held.tile([P, FB], F32, name="b1_col")
+        w2_sb = held.tile([P, FB, C], BF16, name="w2_sb")
+        b2_row = held.tile([P, C], F32, name="b2_row")
         ln_w_col = held.tile([P, CB], F32, name="ln_w_col")
         ln_b_col = held.tile([P, CB], F32, name="ln_b_col")
-        b2_row = held.tile([P, C], F32, name="b2_row")
-        with nc.allow_non_contiguous_dma(reason="small vectors, one float32 to a partition"):
-            nc.sync.dma_start(b1_col[:], b1.rearrange("(fb p) o -> p (fb o)", p=P))
-        nc.sync.dma_start(w1_sb[:, :, W1_FIRST:F], w1_view[:, :, W1_FIRST:F])
-        nc.sync.dma_start(w2_sb[:], w2.rearrange("(fb p) c -> p fb c", p=P))
+        offsets = held.tile([P, N // 16], U16, name="offsets")
+        window = [held.tile([P, S], F32, name=f"window{cb}") for cb in range(CB)]
+        nc.sync.dma_start(x_bf[:], x.rearrange("(cb p) n -> p cb n", p=P))
+        nc.scalar.dma_start(w1_sb[:], w1.rearrange("(cb p) (q fb) -> p cb q fb", p=P, fb=FB))
+        nc.sync.dma_start(b1_col[:], b1.rearrange("(q fb) o -> q (fb o)", fb=FB))
+        nc.sync.dma_start(w2_sb[:], w2.rearrange("(q fb) c -> q fb c", fb=FB))
         nc.sync.dma_start(b2_row[:], b2.rearrange("c o -> (c o)").partition_broadcast(P))
         with nc.allow_non_contiguous_dma(reason="small vectors, one float32 to a partition"):
             nc.sync.dma_start(ln_w_col[:], ln_w.rearrange("(cb p) o -> p (cb o)", p=P))
@@ -70,7 +65,7 @@ def tile_gridtransformerblock_kernel(tc, base, x, w1, b1, w2, b2, ln_w, ln_b, of
             for cb in range(CB):
                 nc.tensor.matmul(
                     h_ps[:],
-                    w1_sb[:, cb, fb * P : (fb + 1) * P],
+                    w1_sb[:, cb, :, fb],
                     x_bf[:, cb, :],
                     start=(cb == 0),
                     stop=(cb == CB - 1),

@@ -4,9 +4,11 @@ from concourse.masks import make_identity
 P = 128
 C, F, S, N = 256, 1024, 4096, 512
 CB, FB, JB = C // P, F // P, N // P
+FG = 4
+FK = FB // FG
 EPS = 1e-5
 FLOPS = 2 * C * F * N * 2
-WARM_UP_MATMULS = 5
+WARM_UP_MATMULS = 3
 
 BF16, F32, U16 = mybir.dt.bfloat16, mybir.dt.float32, mybir.dt.uint16
 ADD, SUB, MULT = mybir.AluOpType.add, mybir.AluOpType.subtract, mybir.AluOpType.mult
@@ -23,7 +25,7 @@ def tile_gridtransformerblock_kernel(tc, base, x, w1, b1, w2, b2, ln_w, ln_b, of
         tc.psum_pool(name="psum_z", bufs=2) as psum_z,
     ):
         x_bf = held.tile([P, CB, N], BF16, name="x_bf")
-        w1_sb = held.tile([P, CB, P, FB], BF16, name="w1_sb")
+        w1_piece = [held.tile([P, CB, P, FK], BF16, name=f"w1_piece{g}") for g in range(FG)]
         b1_col = held.tile([P, FB], F32, name="b1_col")
         w2_sb = held.tile([P, FB, C], BF16, name="w2_sb")
         b2_row = held.tile([P, C], F32, name="b2_row")
@@ -32,9 +34,17 @@ def tile_gridtransformerblock_kernel(tc, base, x, w1, b1, w2, b2, ln_w, ln_b, of
         offsets = held.tile([P, N // 16], U16, name="offsets")
         window = [held.tile([P, S], F32, name=f"window{cb}") for cb in range(CB)]
         nc.sync.dma_start(x_bf[:], x.rearrange("(cb p) n -> p cb n", p=P))
-        nc.scalar.dma_start(w1_sb[:], w1.rearrange("(cb p) (q fb) -> p cb q fb", p=P, fb=FB))
-        nc.sync.dma_start(b1_col[:], b1.rearrange("(q fb) o -> q (fb o)", fb=FB))
-        nc.sync.dma_start(w2_sb[:], w2.rearrange("(q fb) c -> q fb c", fb=FB))
+        w1_view = w1.rearrange("(cb p) (g q k) -> g p cb q k", p=P, g=FG, k=FK)
+        nc.scalar.dma_start(w1_piece[0][:], w1_view[0])
+        with nc.allow_non_contiguous_dma(reason="b1: FK float32 to a partition and piece"):
+            nc.sync.dma_start(
+                b1_col[:].rearrange("q (g k) -> q g k", k=FK), b1.rearrange("(g q k) o -> q g (k o)", g=FG, k=FK)
+            )
+        for g in range(1, FG):
+            nc.sync.dma_start(w1_piece[g][:], w1_view[g])
+        nc.sync.dma_start(
+            w2_sb[:].rearrange("q (g k) c -> q g k c", k=FK), w2.rearrange("(g q k) c -> q g k c", g=FG, k=FK)
+        )
         nc.sync.dma_start(b2_row[:], b2.rearrange("c o -> (c o)").partition_broadcast(P))
         with nc.allow_non_contiguous_dma(reason="small vectors, one float32 to a partition"):
             nc.sync.dma_start(ln_w_col[:], ln_w.rearrange("(cb p) o -> p (cb o)", p=P))
@@ -65,7 +75,7 @@ def tile_gridtransformerblock_kernel(tc, base, x, w1, b1, w2, b2, ln_w, ln_b, of
             for cb in range(CB):
                 nc.tensor.matmul(
                     h_ps[:],
-                    w1_sb[:, cb, :, fb],
+                    w1_piece[fb // FK][:, cb, :, fb % FK],
                     x_bf[:, cb, :],
                     start=(cb == 0),
                     stop=(cb == CB - 1),

@@ -82,7 +82,7 @@ def tile_gridtransformerblock_kernel(tc, base, x, w1, b1, w2, b2, ln_w, ln_b, of
                 )
             nc.scalar.activation(h[:, fb, :], h_ps[:], ACT.Gelu, bias=b1_col[:, fb : fb + 1])
 
-        z = [held.tile([P, N], F32, name=f"z{cb}") for cb in range(CB)]
+        normed = [held.tile([P, C], F32, name=f"normed{jb}") for jb in range(JB)]
         for jb in range(JB):
             pixels = slice(jb * P, (jb + 1) * P)
             y_ps = psum_y.tile([P, C], F32, name="y_ps")
@@ -99,20 +99,29 @@ def tile_gridtransformerblock_kernel(tc, base, x, w1, b1, w2, b2, ln_w, ln_b, of
             nc.vector.bn_aggr(mean_var[:], stats[:])
             rstd = work.tile([P, 1], F32, name="rstd")
             nc.scalar.activation(rstd[:], mean_var[:, 1:2], ACT.Abs_reciprocal_sqrt, bias=eps_col[:, 0:1])
-            normed = work.tile([P, C], F32, name="normed")
-            nc.vector.tensor_scalar(normed[:], y_sb[:], mean_var[:, 0:1], rstd[:, 0:1], SUB, MULT)
-
-            z_ps = psum_z.tile([P, CB, P], F32, name="z_ps")
-            for cb in range(CB):
-                nc.tensor.transpose(z_ps[:, cb, :], normed[:, cb * P : (cb + 1) * P], identity[:])
-                nc.scalar.activation(
-                    z[cb][:, pixels],
-                    z_ps[:, cb, :],
-                    ACT.Identity,
-                    scale=ln_w_col[:, cb : cb + 1],
-                    bias=ln_b_col[:, cb : cb + 1],
-                )
+            nc.vector.tensor_scalar(normed[jb][:], y_sb[:], mean_var[:, 0:1], rstd[:, 0:1], SUB, MULT)
 
         for cb in range(CB):
-            nc.vector.tensor_tensor(window[cb][:].indirect(offsets[:]), x_f32[cb][:], z[cb][:], ADD)
+            z = held.tile([P, N], F32, name=f"z{cb}")
+            for jb in range(JB):
+                z_ps = psum_z.tile([P, P], F32, name="z_ps")
+                nc.tensor.transpose(z_ps[:], normed[jb][:, cb * P : (cb + 1) * P], identity[:])
+                if cb == 0 and jb == JB - 1:
+                    nc.vector.tensor_scalar(
+                        z[:, jb * P : (jb + 1) * P],
+                        z_ps[:],
+                        ln_w_col[:, cb : cb + 1],
+                        ln_b_col[:, cb : cb + 1],
+                        MULT,
+                        ADD,
+                    )
+                else:
+                    nc.scalar.activation(
+                        z[:, jb * P : (jb + 1) * P],
+                        z_ps[:],
+                        ACT.Identity,
+                        scale=ln_w_col[:, cb : cb + 1],
+                        bias=ln_b_col[:, cb : cb + 1],
+                    )
+            nc.vector.tensor_tensor(window[cb][:].indirect(offsets[:]), x_f32[cb][:], z[:], ADD)
             nc.sync.dma_start(out[cb * P : (cb + 1) * P, :], window[cb][:])

@@ -83,15 +83,29 @@ def tile_gridtransformerblock_kernel(tc, base, x, w1, b1, w2, b2, ln_w, ln_b, of
             nc.scalar.activation(h[:, fb, :], h_ps[:], ACT.Gelu, bias=b1_col[:, fb : fb + 1])
 
         normed = [held.tile([P, C], F32, name=f"normed{jb}") for jb in range(JB)]
-        for jb in range(JB):
-            pixels = slice(jb * P, (jb + 1) * P)
-            y_ps = psum_y.tile([P, C], F32, name="y_ps")
-            for fb in range(FB):
+        y_ps = [None] * JB
+        written = [0] * JB
+
+        def products(jb, upto):
+            if written[jb] == 0:
+                y_ps[jb] = psum_y.tile([P, C], F32, name="y_ps")
+            for fb in range(written[jb], upto):
                 nc.tensor.matmul(
-                    y_ps[:], h[:, fb, pixels], w2_sb[:, fb, :], start=(fb == 0), stop=(fb == FB - 1)
+                    y_ps[jb][:],
+                    h[:, fb, jb * P : (jb + 1) * P],
+                    w2_sb[:, fb, :],
+                    start=(fb == 0),
+                    stop=(fb == FB - 1),
                 )
+            written[jb] = upto
+
+        for jb in range(JB):
+            if jb == 0:
+                products(0, FB - 1)
+                products(1, FB // 2)
+            products(jb, FB)
             y_sb = work.tile([P, C], F32, name="y_sb")
-            nc.vector.tensor_tensor(y_sb[:], y_ps[:], b2_row[:], ADD)
+            nc.vector.tensor_tensor(y_sb[:], y_ps[jb][:], b2_row[:], ADD)
 
             stats = work.tile([P, 6], F32, name="stats")
             nc.vector.bn_stats(stats[:], y_sb[:])

@@ -24,7 +24,7 @@ def tile_gridtransformerblock_kernel(tc, base, x, w1, b1, w2, b2, ln_w, ln_b, of
         tc.psum_pool(name="psum_y", bufs=2) as psum_y,
         tc.psum_pool(name="psum_z", bufs=2) as psum_z,
     ):
-        x_bf = held.tile([P, CB, N], BF16, name="x_bf")
+        x_bf = [held.tile([P, N], BF16, name=f"x_bf{cb}") for cb in range(CB)]
         w1_piece = [held.tile([P, CB, P, FK], BF16, name=f"w1_piece{g}") for g in range(FG)]
         b1_col = held.tile([P, FB], F32, name="b1_col")
         w2_sb = held.tile([P, FB, C], BF16, name="w2_sb")
@@ -33,9 +33,10 @@ def tile_gridtransformerblock_kernel(tc, base, x, w1, b1, w2, b2, ln_w, ln_b, of
         ln_b_col = held.tile([P, CB], F32, name="ln_b_col")
         offsets = held.tile([P, N // 16], U16, name="offsets")
         window = [held.tile([P, S], F32, name=f"window{cb}") for cb in range(CB)]
-        nc.sync.dma_start(x_bf[:], x.rearrange("(cb p) n -> p cb n", p=P))
+        nc.sync.dma_start(x_bf[0][:], x[0:P, :])
         w1_view = w1.rearrange("(cb p) (g q k) -> g p cb q k", p=P, g=FG, k=FK)
         nc.scalar.dma_start(w1_piece[0][:], w1_view[0])
+        nc.sync.dma_start(x_bf[1][:], x[P:C, :])
         with nc.allow_non_contiguous_dma(reason="b1: FK float32 to a partition and piece"):
             nc.sync.dma_start(
                 b1_col[:].rearrange("q (g k) -> q g k", k=FK), b1.rearrange("(g q k) o -> q g (k o)", g=FG, k=FK)
@@ -67,7 +68,7 @@ def tile_gridtransformerblock_kernel(tc, base, x, w1, b1, w2, b2, ln_w, ln_b, of
 
         x_f32 = [held.tile([P, N], F32, name=f"x_f32_{cb}") for cb in range(CB)]
         for cb in range(CB):
-            nc.gpsimd.tensor_copy(x_f32[cb][:], x_bf[:, cb, :])
+            nc.gpsimd.tensor_copy(x_f32[cb][:], x_bf[cb][:])
 
         h = held.tile([P, FB, N], BF16, name="h")
         for fb in range(FB):
@@ -76,7 +77,7 @@ def tile_gridtransformerblock_kernel(tc, base, x, w1, b1, w2, b2, ln_w, ln_b, of
                 nc.tensor.matmul(
                     h_ps[:],
                     w1_piece[fb // FK][:, cb, :, fb % FK],
-                    x_bf[:, cb, :],
+                    x_bf[cb][:],
                     start=(cb == 0),
                     stop=(cb == CB - 1),
                 )

@@ -8,7 +8,7 @@ FG = 4
 FK = FB // FG
 EPS = 1e-5
 FLOPS = 2 * C * F * N * 2
-WARM_UP_MATMULS = 3
+WARM_UP_MATMULS = 12
 
 BF16, F32, U16 = mybir.dt.bfloat16, mybir.dt.float32, mybir.dt.uint16
 ADD, SUB, MULT = mybir.AluOpType.add, mybir.AluOpType.subtract, mybir.AluOpType.mult
@@ -53,14 +53,15 @@ def tile_gridtransformerblock_kernel(tc, base, x, w1, b1, w2, b2, ln_w, ln_b, of
         nc.sync.dma_start(offsets[:], offs)
         for cb in range(CB):
             nc.sync.dma_start(window[cb][:], base[cb * P : (cb + 1) * P, :])
-        identity = held.tile([P, P], F32, name="identity")
-        make_identity(nc, identity[:])
 
-        zeros = held.tile([P, N], BF16, name="zeros")
+        zeros = held.tile([P, P], BF16, name="zeros")
         nc.vector.memset(zeros[:], 0.0)
         warm_ps = psum_h.tile([P, N], F32, name="warm_ps", tag="h_ps")
         for repeat in range(WARM_UP_MATMULS):
-            nc.tensor.matmul(warm_ps[:], zeros[:, 0:P], zeros[:], start=True, stop=True)
+            nc.tensor.matmul(warm_ps[:, 0:P], zeros[:], zeros[:], start=True, stop=True)
+        identity = held.tile([P, P], F32, name="identity")
+        nc.vector.memset(identity[:], 0.0)
+        make_identity(nc, identity[:], nomemset=True)
         eps_col = held.tile([P, 1], F32, name="eps_col")
         nc.vector.memset(eps_col[:], EPS)
         scratch_col = held.tile([P, 1], F32, name="scratch_col")

@@ -20,9 +20,8 @@ def tile_gridtransformerblock_kernel(tc, base, x, w1, b1, w2, b2, ln_w, ln_b, of
     with (
         tc.tile_pool(name="held", bufs=1) as held,
         tc.tile_pool(name="work", bufs=2) as work,
-        tc.psum_pool(name="psum_h", bufs=3) as psum_h,
-        tc.psum_pool(name="psum_y", bufs=2) as psum_y,
-        tc.psum_pool(name="psum_z", bufs=2) as psum_z,
+        tc.psum_pool(name="psum_h", bufs=4) as psum_h,
+        tc.psum_pool(name="psum_y", bufs=JB) as psum_y,
     ):
         x_bf = [held.tile([P, N], BF16, name=f"x_bf{cb}") for cb in range(CB)]
         w1_piece = [held.tile([P, CB, P, FK], BF16, name=f"w1_piece{g}") for g in range(FG)]
@@ -43,10 +42,10 @@ def tile_gridtransformerblock_kernel(tc, base, x, w1, b1, w2, b2, ln_w, ln_b, of
             )
         for g in range(1, FG):
             nc.sync.dma_start(w1_piece[g][:], w1_view[g])
+        nc.sync.dma_start(b2_row[:], b2.rearrange("c o -> (c o)").partition_broadcast(P))
         nc.sync.dma_start(
             w2_sb[:].rearrange("q (g k) c -> q g k c", k=FK), w2.rearrange("(g q k) c -> q g k c", g=FG, k=FK)
         )
-        nc.sync.dma_start(b2_row[:], b2.rearrange("c o -> (c o)").partition_broadcast(P))
         with nc.allow_non_contiguous_dma(reason="small vectors, one float32 to a partition"):
             nc.sync.dma_start(ln_w_col[:], ln_w.rearrange("(cb p) o -> p (cb o)", p=P))
             nc.sync.dma_start(ln_b_col[:], ln_b.rearrange("(cb p) o -> p (cb o)", p=P))
@@ -67,6 +66,19 @@ def tile_gridtransformerblock_kernel(tc, base, x, w1, b1, w2, b2, ln_w, ln_b, of
         scratch_col = held.tile([P, 1], F32, name="scratch_col")
         nc.scalar.activation(scratch_col[:], eps_col[:], ACT.Gelu)
 
+        b2_parts = held.tile([P, C], BF16, name="b2_parts")
+        rest = held.tile([P, C], F32, name="rest")
+        rest_lo = held.tile([P, C], F32, name="rest_lo")
+        nc.vector.tensor_copy(b2_parts[:], b2_row[:])
+        nc.vector.tensor_tensor(rest[:], b2_row[:], b2_parts[:], SUB)
+        nc.vector.tensor_copy(b2_parts[32:64, :], rest[32:64, :])
+        nc.vector.tensor_copy(b2_parts[64:P, :], rest[64:P, :])
+        nc.vector.tensor_tensor(rest_lo[64:P, :], rest[64:P, :], b2_parts[64:P, :], SUB)
+        nc.vector.tensor_copy(b2_parts[64:P, :], rest_lo[64:P, :])
+        share = held.tile([P, P], BF16, name="share")
+        nc.vector.memset(share[0:64, :], 1 / 32)
+        nc.vector.memset(share[64:P, :], 1 / 64)
+
         x_f32 = [held.tile([P, N], F32, name=f"x_f32_{cb}") for cb in range(CB)]
         for cb in range(CB):
             nc.gpsimd.tensor_copy(x_f32[cb][:], x_bf[cb][:])
@@ -84,19 +96,20 @@ def tile_gridtransformerblock_kernel(tc, base, x, w1, b1, w2, b2, ln_w, ln_b, of
                 )
             nc.scalar.activation(h[:, fb, :], h_ps[:], ACT.Gelu, bias=b1_col[:, fb : fb + 1])
 
-        normed = [held.tile([P, C], F32, name=f"normed{jb}") for jb in range(JB)]
+        normed = [[held.tile([P, P], F32, name=f"normed{jb}_{cb}") for cb in range(CB)] for jb in range(JB)]
         y_ps = [None] * JB
         written = [0] * JB
 
         def products(jb, upto):
             if written[jb] == 0:
                 y_ps[jb] = psum_y.tile([P, C], F32, name="y_ps")
+                nc.tensor.matmul(y_ps[jb][:], share[:], b2_parts[:], start=True, stop=False)
             for fb in range(written[jb], upto):
                 nc.tensor.matmul(
                     y_ps[jb][:],
                     h[:, fb, jb * P : (jb + 1) * P],
                     w2_sb[:, fb, :],
-                    start=(fb == 0),
+                    start=False,
                     stop=(fb == FB - 1),
                 )
             written[jb] = upto
@@ -106,22 +119,28 @@ def tile_gridtransformerblock_kernel(tc, base, x, w1, b1, w2, b2, ln_w, ln_b, of
                 products(0, FB - 1)
                 products(1, FB // 2)
             products(jb, FB)
-            y_sb = work.tile([P, C], F32, name="y_sb")
-            nc.vector.tensor_tensor(y_sb[:], y_ps[jb][:], b2_row[:], ADD)
 
             stats = work.tile([P, 6], F32, name="stats")
-            nc.vector.bn_stats(stats[:], y_sb[:])
+            nc.vector.bn_stats(stats[:], y_ps[jb][:])
             mean_var = work.tile([P, 2], F32, name="mean_var")
             nc.vector.bn_aggr(mean_var[:], stats[:])
             rstd = work.tile([P, 1], F32, name="rstd")
             nc.scalar.activation(rstd[:], mean_var[:, 1:2], ACT.Abs_reciprocal_sqrt, bias=eps_col[:, 0:1])
-            nc.vector.tensor_scalar(normed[jb][:], y_sb[:], mean_var[:, 0:1], rstd[:, 0:1], SUB, MULT)
+            for cb in range(CB):
+                nc.vector.tensor_scalar(
+                    normed[jb][cb][:],
+                    y_ps[jb][:, cb * P : (cb + 1) * P],
+                    mean_var[:, 0:1],
+                    rstd[:, 0:1],
+                    SUB,
+                    MULT,
+                )
 
         for cb in range(CB):
             z = held.tile([P, N], F32, name=f"z{cb}")
             for jb in range(JB):
-                z_ps = psum_z.tile([P, P], F32, name="z_ps")
-                nc.tensor.transpose(z_ps[:], normed[jb][:, cb * P : (cb + 1) * P], identity[:])
+                z_ps = psum_h.tile([P, P], F32, name="z_ps", tag="h_ps")
+                nc.tensor.transpose(z_ps[:], normed[jb][cb][:], identity[:])
                 if cb == 0 and jb == JB - 1:
                     nc.vector.tensor_scalar(
                         z[:, jb * P : (jb + 1) * P],

@@ -27,11 +27,14 @@ def tile_gridtransformerblock_kernel(tc, base, x, w1, b1, w2, b2, ln_w, ln_b, of
         w1_piece = [held.tile([P, CB, P, FK], BF16, name=f"w1_piece{g}") for g in range(FG)]
         b1_col = held.tile([P, FB], F32, name="b1_col")
         w2_sb = held.tile([P, FB, C], BF16, name="w2_sb")
-        b2_row = held.tile([P, C], F32, name="b2_row")
+        b2_rows = held.tile([P, C], F32, name="b2_rows")
         ln_w_col = held.tile([P, CB], F32, name="ln_w_col")
         ln_b_col = held.tile([P, CB], F32, name="ln_b_col")
         offsets = held.tile([P, N // 16], U16, name="offsets")
         window = [held.tile([P, S], F32, name=f"window{cb}") for cb in range(CB)]
+        zeros = held.tile([P, P], BF16, name="zeros")
+        nc.vector.memset(zeros[:], 0.0)
+        nc.vector.memset(b2_rows[:], 0.0)
         nc.sync.dma_start(x_bf[0][:], x[0:P, :])
         w1_view = w1.rearrange("(cb p) (g q k) -> g p cb q k", p=P, g=FG, k=FK)
         nc.scalar.dma_start(w1_piece[0][:], w1_view[0])
@@ -40,9 +43,12 @@ def tile_gridtransformerblock_kernel(tc, base, x, w1, b1, w2, b2, ln_w, ln_b, of
             nc.sync.dma_start(
                 b1_col[:].rearrange("q (g k) -> q g k", k=FK), b1.rearrange("(g q k) o -> q g (k o)", g=FG, k=FK)
             )
+        nc.sync.dma_start(
+            b2_rows[:].rearrange("(quadrant p) c -> p quadrant c", p=32)[0],
+            b2.rearrange("c o -> (c o)").partition_broadcast(P // 32),
+        )
         for g in range(1, FG):
             nc.sync.dma_start(w1_piece[g][:], w1_view[g])
-        nc.sync.dma_start(b2_row[:], b2.rearrange("c o -> (c o)").partition_broadcast(P))
         nc.sync.dma_start(
             w2_sb[:].rearrange("q (g k) c -> q g k c", k=FK), w2.rearrange("(g q k) c -> q g k c", g=FG, k=FK)
         )
@@ -53,8 +59,6 @@ def tile_gridtransformerblock_kernel(tc, base, x, w1, b1, w2, b2, ln_w, ln_b, of
         for cb in range(CB):
             nc.sync.dma_start(window[cb][:], base[cb * P : (cb + 1) * P, :])
 
-        zeros = held.tile([P, P], BF16, name="zeros")
-        nc.vector.memset(zeros[:], 0.0)
         warm_ps = psum_h.tile([P, N], F32, name="warm_ps", tag="h_ps")
         for repeat in range(WARM_UP_MATMULS):
             nc.tensor.matmul(warm_ps[:, 0:P], zeros[:], zeros[:], start=True, stop=True)
@@ -69,15 +73,15 @@ def tile_gridtransformerblock_kernel(tc, base, x, w1, b1, w2, b2, ln_w, ln_b, of
         b2_parts = held.tile([P, C], BF16, name="b2_parts")
         rest = held.tile([P, C], F32, name="rest")
         rest_lo = held.tile([P, C], F32, name="rest_lo")
-        nc.vector.tensor_copy(b2_parts[:], b2_row[:])
-        nc.vector.tensor_tensor(rest[:], b2_row[:], b2_parts[:], SUB)
+        nc.vector.tensor_copy(b2_parts[:], b2_rows[:])
+        nc.vector.tensor_tensor(rest[:], b2_rows[:], b2_parts[:], SUB)
         nc.vector.tensor_copy(b2_parts[32:64, :], rest[32:64, :])
         nc.vector.tensor_copy(b2_parts[64:P, :], rest[64:P, :])
         nc.vector.tensor_tensor(rest_lo[64:P, :], rest[64:P, :], b2_parts[64:P, :], SUB)
         nc.vector.tensor_copy(b2_parts[64:P, :], rest_lo[64:P, :])
         share = held.tile([P, P], BF16, name="share")
-        nc.vector.memset(share[0:64, :], 1 / 32)
-        nc.vector.memset(share[64:P, :], 1 / 64)
+        nc.vector.memset(share[0:64, :], 1.0)
+        nc.vector.memset(share[64:P, :], 0.5)
 
         x_f32 = [held.tile([P, N], F32, name=f"x_f32_{cb}") for cb in range(CB)]
         for cb in range(CB):

@@ -40,7 +40,7 @@ def tile_gridtransformerblock_kernel(tc, base, x, w1, b1, w2, b2, ln_w, ln_b, of
         nc.scalar.dma_start(w1_piece[0][:], w1_view[0])
         nc.sync.dma_start(x_bf[1][:], x[P:C, :])
         with nc.allow_non_contiguous_dma(reason="b1: FK float32 to a partition and piece"):
-            nc.sync.dma_start(
+            nc.scalar.dma_start(
                 b1_col[:].rearrange("q (g k) -> q g k", k=FK), b1.rearrange("(g q k) o -> q g (k o)", g=FG, k=FK)
             )
         nc.sync.dma_start(

@@ -125,16 +125,17 @@ def tile_gridtransformerblock_kernel(tc, base, x, w1, b1, w2, b2, ln_w, ln_b, of
             products(jb, FB)
 
             stats = work.tile([P, 6], F32, name="stats")
-            nc.vector.bn_stats(stats[:], y_ps[jb][:])
-            mean_var = work.tile([P, 2], F32, name="mean_var")
-            nc.vector.bn_aggr(mean_var[:], stats[:])
+            nc.vector.bn_stats(stats[:], y_ps[jb][:].unsqueeze(2).to_broadcast([P, C, 2]))
+            mean = stats[:, 1:2]
             rstd = work.tile([P, 1], F32, name="rstd")
-            nc.scalar.activation(rstd[:], mean_var[:, 1:2], ACT.Abs_reciprocal_sqrt, bias=eps_col[:, 0:1])
+            nc.scalar.activation(
+                rstd[:], stats[:, 2:3], ACT.Abs_reciprocal_sqrt, scale=1 / C, bias=eps_col[:, 0:1]
+            )
             for cb in range(CB):
                 nc.vector.tensor_scalar(
                     normed[jb][cb][:],
                     y_ps[jb][:, cb * P : (cb + 1) * P],
-                    mean_var[:, 0:1],
+                    mean,
                     rstd[:, 0:1],
                     SUB,
                     MULT,

import concourse.mybir as mybir
from concourse.masks import make_identity

P = 128
C, F, S, N = 256, 1024, 4096, 512
CB, FB, JB = C // P, F // P, N // P
FG = 4
FK = FB // FG
EPS = 1e-5
FLOPS = 2 * C * F * N * 2
WARM_UP_MATMULS = 12

BF16, F32, U16 = mybir.dt.bfloat16, mybir.dt.float32, mybir.dt.uint16
ADD, SUB, MULT = mybir.AluOpType.add, mybir.AluOpType.subtract, mybir.AluOpType.mult
ACT = mybir.ActivationFunctionType


def tile_gridtransformerblock_kernel(tc, base, x, w1, b1, w2, b2, ln_w, ln_b, offs, out):
    nc = tc.nc
    with (
        tc.tile_pool(name="held", bufs=1) as held,
        tc.tile_pool(name="work", bufs=2) as work,
        tc.psum_pool(name="psum_h", bufs=4) as psum_h,
        tc.psum_pool(name="psum_y", bufs=JB) as psum_y,
    ):
        x_bf = [held.tile([P, N], BF16, name=f"x_bf{cb}") for cb in range(CB)]
        w1_piece = [held.tile([P, CB, P, FK], BF16, name=f"w1_piece{g}") for g in range(FG)]
        b1_col = held.tile([P, FB], F32, name="b1_col")
        w2_sb = held.tile([P, FB, C], BF16, name="w2_sb")
        b2_rows = held.tile([P, C], F32, name="b2_rows")
        ln_w_col = held.tile([P, CB], F32, name="ln_w_col")
        ln_b_col = held.tile([P, CB], F32, name="ln_b_col")
        offsets = held.tile([P, N // 16], U16, name="offsets")
        window = [held.tile([P, S], F32, name=f"window{cb}") for cb in range(CB)]
        zeros = held.tile([P, P], BF16, name="zeros")
        nc.vector.memset(zeros[:], 0.0)
        nc.vector.memset(b2_rows[:], 0.0)
        nc.sync.dma_start(x_bf[0][:], x[0:P, :])
        w1_view = w1.rearrange("(cb p) (g q k) -> g p cb q k", p=P, g=FG, k=FK)
        nc.scalar.dma_start(w1_piece[0][:], w1_view[0])
        nc.sync.dma_start(x_bf[1][:], x[P:C, :])
        with nc.allow_non_contiguous_dma(reason="b1: FK float32 to a partition and piece"):
            nc.scalar.dma_start(
                b1_col[:].rearrange("q (g k) -> q g k", k=FK), b1.rearrange("(g q k) o -> q g (k o)", g=FG, k=FK)
            )
        nc.sync.dma_start(
            b2_rows[:].rearrange("(quadrant p) c -> p quadrant c", p=32)[0],
            b2.rearrange("c o -> (c o)").partition_broadcast(P // 32),
        )
        for g in range(1, FG):
            nc.sync.dma_start(w1_piece[g][:], w1_view[g])
        nc.sync.dma_start(
            w2_sb[:].rearrange("q (g k) c -> q g k c", k=FK), w2.rearrange("(g q k) c -> q g k c", g=FG, k=FK)
        )
        with nc.allow_non_contiguous_dma(reason="small vectors, one float32 to a partition"):
            nc.sync.dma_start(ln_w_col[:], ln_w.rearrange("(cb p) o -> p (cb o)", p=P))
            nc.sync.dma_start(ln_b_col[:], ln_b.rearrange("(cb p) o -> p (cb o)", p=P))
        nc.sync.dma_start(offsets[:], offs)
        for cb in range(CB):
            nc.sync.dma_start(window[cb][:], base[cb * P : (cb + 1) * P, :])

        warm_ps = psum_h.tile([P, N], F32, name="warm_ps", tag="h_ps")
        for repeat in range(WARM_UP_MATMULS):
            nc.tensor.matmul(warm_ps[:, 0:P], zeros[:], zeros[:], start=True, stop=True)
        identity = held.tile([P, P], F32, name="identity")
        nc.vector.memset(identity[:], 0.0)
        make_identity(nc, identity[:], nomemset=True)
        eps_col = held.tile([P, 1], F32, name="eps_col")
        nc.vector.memset(eps_col[:], EPS)
        scratch_col = held.tile([P, 1], F32, name="scratch_col")
        nc.scalar.activation(scratch_col[:], eps_col[:], ACT.Gelu)

        b2_parts = held.tile([P, C], BF16, name="b2_parts")
        rest = held.tile([P, C], F32, name="rest")
        rest_lo = held.tile([P, C], F32, name="rest_lo")
        nc.vector.tensor_copy(b2_parts[:], b2_rows[:])
        nc.vector.tensor_tensor(rest[:], b2_rows[:], b2_parts[:], SUB)
        nc.vector.tensor_copy(b2_parts[32:64, :], rest[32:64, :])
        nc.vector.tensor_copy(b2_parts[64:P, :], rest[64:P, :])
        nc.vector.tensor_tensor(rest_lo[64:P, :], rest[64:P, :], b2_parts[64:P, :], SUB)
        nc.vector.tensor_copy(b2_parts[64:P, :], rest_lo[64:P, :])
        share = held.tile([P, P], BF16, name="share")
        nc.vector.memset(share[0:64, :], 1.0)
        nc.vector.memset(share[64:P, :], 0.5)

        x_f32 = [held.tile([P, N], F32, name=f"x_f32_{cb}") for cb in range(CB)]
        for cb in range(CB):
            nc.gpsimd.tensor_copy(x_f32[cb][:], x_bf[cb][:])

        h = held.tile([P, FB, N], BF16, name="h")
        for fb in range(FB):
            h_ps = psum_h.tile([P, N], F32, name="h_ps")
            for cb in range(CB):
                nc.tensor.matmul(
                    h_ps[:],
                    w1_piece[fb // FK][:, cb, :, fb % FK],
                    x_bf[cb][:],
                    start=(cb == 0),
                    stop=(cb == CB - 1),
                )
            nc.scalar.activation(h[:, fb, :], h_ps[:], ACT.Gelu, bias=b1_col[:, fb : fb + 1])

        normed = [[held.tile([P, P], F32, name=f"normed{jb}_{cb}") for cb in range(CB)] for jb in range(JB)]
        y_ps = [None] * JB
        written = [0] * JB

        def products(jb, upto):
            if written[jb] == 0:
                y_ps[jb] = psum_y.tile([P, C], F32, name="y_ps")
                nc.tensor.matmul(y_ps[jb][:], share[:], b2_parts[:], start=True, stop=False)
            for fb in range(written[jb], upto):
                nc.tensor.matmul(
                    y_ps[jb][:],
                    h[:, fb, jb * P : (jb + 1) * P],
                    w2_sb[:, fb, :],
                    start=False,
                    stop=(fb == FB - 1),
                )
            written[jb] = upto

        for jb in range(JB):
            if jb == 0:
                products(0, FB - 1)
                products(1, FB // 2)
            products(jb, FB)

            stats = work.tile([P, 6], F32, name="stats")
            nc.vector.bn_stats(stats[:], y_ps[jb][:].unsqueeze(2).to_broadcast([P, C, 2]))
            mean = stats[:, 1:2]
            rstd = work.tile([P, 1], F32, name="rstd")
            nc.scalar.activation(
                rstd[:], stats[:, 2:3], ACT.Abs_reciprocal_sqrt, scale=1 / C, bias=eps_col[:, 0:1]
            )
            for cb in range(CB):
                nc.vector.tensor_scalar(
                    normed[jb][cb][:],
                    y_ps[jb][:, cb * P : (cb + 1) * P],
                    mean,
                    rstd[:, 0:1],
                    SUB,
                    MULT,
                )

        for cb in range(CB):
            z = held.tile([P, N], F32, name=f"z{cb}")
            for jb in range(JB):
                z_ps = psum_h.tile([P, P], F32, name="z_ps", tag="h_ps")
                nc.tensor.transpose(z_ps[:], normed[jb][cb][:], identity[:])
                if cb == 0 and jb == JB - 1:
                    nc.vector.tensor_scalar(
                        z[:, jb * P : (jb + 1) * P],
                        z_ps[:],
                        ln_w_col[:, cb : cb + 1],
                        ln_b_col[:, cb : cb + 1],
                        MULT,
                        ADD,
                    )
                else:
                    nc.scalar.activation(
                        z[:, jb * P : (jb + 1) * P],
                        z_ps[:],
                        ACT.Identity,
                        scale=ln_w_col[:, cb : cb + 1],
                        bias=ln_b_col[:, cb : cb + 1],
                    )
            nc.vector.tensor_tensor(window[cb][:].indirect(offsets[:]), x_f32[cb][:], z[:], ADD)
            nc.sync.dma_start(out[cb * P : (cb + 1) * P, :], window[cb][:])
